import numpy as np
import ml_dtypes


def mxq(x, axis, fmt="e4m3"):
    dtype, down = {"e4m3": (ml_dtypes.float8_e4m3fn, 7), "e5m2": (ml_dtypes.float8_e5m2, 14)}[fmt]
    v = np.moveaxis(np.asarray(x, np.float32).astype(ml_dtypes.bfloat16).astype(np.float64), axis, -1)
    blocks = v.reshape(v.shape[:-1] + (-1, 32))
    amax = np.abs(blocks).max(-1, keepdims=True)
    byte = np.maximum(np.where(amax > 0, np.frexp(amax)[1] - 1 + 127, 0) - down, 1)
    scale = np.exp2(byte - 127.0)
    codes = (blocks / scale).astype(np.float32).astype(dtype).astype(np.float64)
    return np.moveaxis((codes * scale).reshape(v.shape), -1, axis)


WIDE = False


def mx_kscale(k):
    if not WIDE:
        return np.ones(k)
    levels = np.array([10, -10, 5, -5, 0])
    a = np.random.permutation(np.resize(levels, k // 512 * 4)).reshape(k // 512, 4)
    idx = np.arange(k)
    return np.exp2(a[idx // 512, idx % 128 // 32])


BF16 = ml_dtypes.bfloat16


def bf(x):
    return np.asarray(x, np.float32).astype(BF16)


def f64(x):
    return np.asarray(x).astype(np.float64)


B, N, D, F = 4, 64, 512, 128


def setup_inputs():
    s, t = mx_kscale(D), mx_kscale(D)
    ss = np.concatenate([s, s])
    sst = np.concatenate([s, s, t])
    return {
        'text_embedding': bf(np.random.standard_normal((B, N, D)) * s),
        'W_rel': bf(np.random.standard_normal((2 * D, D)) / np.sqrt(2 * D) / ss[:, None] * t),
        'b_rel': bf(np.random.standard_normal(D) * 0.3 * t),
        'W_go': bf(np.random.standard_normal((D, D)) / np.sqrt(D) / s[:, None]),
        'b_go': bf(np.random.standard_normal(D) * 0.3),
        'W_gr': bf(np.random.standard_normal((3 * D, F)) * 1.5 / np.sqrt(3 * D) / sst[:, None]),
        'b_gr': bf(np.random.standard_normal(F) * 0.3),
    }


def reference(text_embedding, W_rel, b_rel, W_go, b_go, W_gr, b_gr):
    xq = mxq(f64(text_embedding), 2, 'e4m3')
    wr, wg = f64(W_rel), f64(W_gr)
    new_x = np.tanh((xq @ mxq(f64(W_go), 0, 'e4m3')) + f64(b_go))
    rel0 = ((xq @ mxq(wr[:D], 0, 'e4m3'))[:, :, None, :]
            + (xq @ mxq(wr[D:], 0, 'e4m3'))[:, None, :, :] + f64(b_rel))
    pre = ((xq @ mxq(wg[:D], 0, 'e4m3'))[:, :, None, :]
           + (xq @ mxq(wg[D:2 * D], 0, 'e4m3'))[:, None, :, :]
           + (mxq(rel0, 3, 'e4m3') @ mxq(wg[2 * D:], 0, 'e4m3')) + f64(b_gr))
    return new_x, np.tanh(pre)

@@ -1,0 +1,240 @@
+from contextlib import ExitStack
+
+import concourse.mybir as mybir
+from concourse.masks import make_identity
+
+F32 = mybir.dt.float32
+BF16 = mybir.dt.bfloat16
+I32 = mybir.dt.int32
+U8 = mybir.dt.uint8
+FP8X4 = mybir.dt.float8_e4m3fn_x4
+ADD = mybir.AluOpType.add
+ACT = mybir.ActivationFunctionType
+
+P = 128
+FLOPS = 2 * 256 * 512 * (3 * 512 + 2 * 128) + 2 * 16384 * 512 * 128
+
+
+def tile_languagemsgencoder_pa_t_kernel(
+    tc, text_embedding, W_rel, b_rel, W_go, b_go, W_gr, b_gr, out_0, out_1
+):
+    nc = tc.nc
+    out0_flat = out_0.rearrange("b n d -> (b n) d")
+    out1_flat = out_1.rearrange("b i j f -> (b i j) f")
+
+    def mx(out, l_codes, l_scales, r_codes, r_scales, start, stop):
+        nc.tensor.matmul_mx(
+            out=out,
+            lhsT=l_codes.bitcast(FP8X4),
+            lhsT_scale=l_scales,
+            rhs=r_codes.bitcast(FP8X4),
+            rhs_scale=r_scales,
+            start=start,
+            stop=stop,
+        )
+
+    def quantise(codes, scales, grouped):
+        nc.vector.quantize_mx(out=codes.bitcast(FP8X4), scales=scales, in_=grouped)
+
+    def regroup_views(dst, src):
+        return (
+            dst.rearrange("p (c i) t -> p c t i", i=4),
+            src.rearrange("p t (c i) -> p c t i", i=4),
+        )
+
+    with ExitStack() as ctx:
+        const = ctx.enter_context(tc.tile_pool(name="const", bufs=1))
+        relp = ctx.enter_context(tc.tile_pool(name="relp", bufs=3))
+        outp = ctx.enter_context(tc.tile_pool(name="outp", bufs=4))
+        thp = ctx.enter_context(tc.tile_pool(name="thp", bufs=6))
+        atp = ctx.enter_context(tc.psum_pool(name="atp", bufs=1))
+        hd = ctx.enter_context(tc.psum_pool(name="hd", bufs=2))
+        accp = ctx.enter_context(tc.psum_pool(name="accp", bufs=2))
+        trp = ctx.enter_context(tc.psum_pool(name="trp", bufs=2))
+
+        x_sb = const.tile([P, 2, 512], BF16)
+        wrel_raw = const.tile([P, 8, 512], BF16)
+        wgr_raw = const.tile([P, 12, 128], BF16)
+        wgo_raw = const.tile([P, 4, 512], BF16)
+        bias_rows = const.tile([P, P], BF16)
+        x_scales = const.tile([P, 256], U8, align_bytes=64)
+
+        nc.vector.memset(bias_rows[:], 0.0)
+        nc.vector.memset(x_scales[:].bitcast(I32), 0)
+
+        nc.sync.dma_start(
+            out=x_sb[:],
+            in_=text_embedding.rearrange("b n d -> (b n) d").rearrange("(a p) d -> p a d", p=P),
+        )
+        nc.sync.dma_start(out=wrel_raw[:, 0:4, :], in_=W_rel[0:512, :].rearrange("(t p) c -> p t c", p=P))
+        nc.sync.dma_start(out=wrel_raw[:, 4:8, :], in_=W_rel[512:1024, :].rearrange("(t p) c -> p t c", p=P))
+        nc.scalar.dma_start(out=bias_rows[0:4, :], in_=b_rel.rearrange("(t p) -> t p", p=P))
+        nc.scalar.dma_start(out=bias_rows[4:8, :], in_=b_go.rearrange("(t p) -> t p", p=P))
+        nc.scalar.dma_start(out=bias_rows[8:9, :], in_=b_gr.rearrange("(o p) -> o p", o=1))
+        nc.sync.dma_start(out=wgr_raw[:], in_=W_gr.rearrange("(h p) c -> p h c", p=P))
+        nc.sync.dma_start(out=wgo_raw[:], in_=W_go.rearrange("(t p) c -> p t c", p=P))
+
+        ident_bf = const.tile([P, P], BF16)
+        make_identity(nc, ident_bf[:])
+        ident_f = const.tile([P, P], F32)
+        make_identity(nc, ident_f[:])
+
+        xt_ps = hd.tile([P, 4, 256], BF16, tag="hd")
+        for a in range(2):
+            for t in range(4):
+                nc.tensor.transpose(
+                    xt_ps[:, t, a * P:(a + 1) * P], x_sb[:, a, t * P:(t + 1) * P], ident_bf[:]
+                )
+        x_grp = const.tile([P, 256, 4], BF16, align_bytes=64)
+        x_codes = const.tile([P, 256], I32, align_bytes=64)
+        nc.vector.tensor_copy(out=x_grp[:], in_=xt_ps[:].rearrange("p t n -> p n t"))
+
+        b_ps = hd.tile([P, P], BF16, tag="hd")
+        nc.tensor.transpose(b_ps[:], bias_rows[:], ident_bf[:])
+        bias_sb = const.tile([P, 16], F32)
+        nc.scalar.copy(out=bias_sb[:], in_=b_ps[:, 0:16])
+
+        wrel_grp = const.tile([P, 2, 512, 4], BF16, align_bytes=64)
+        wrel_codes = const.tile([P, 2, 512], I32, align_bytes=64)
+        wrel_scales = const.tile([P, 2, 512], U8, align_bytes=64)
+        SPLIT = 320
+        for h in range(2):
+            d, s = regroup_views(wrel_grp[:, h, 0:SPLIT, :], wrel_raw[:, 4 * h:4 * h + 4, 0:SPLIT])
+            nc.vector.tensor_copy(out=d, in_=s)
+            d, s = regroup_views(wrel_grp[:, h, SPLIT:512, :], wrel_raw[:, 4 * h:4 * h + 4, SPLIT:512])
+            nc.scalar.copy(out=d, in_=s)
+        quantise(x_codes[:], x_scales[:], x_grp[:].rearrange("p n t -> p (n t)"))
+        for h in range(2):
+            quantise(wrel_codes[:, h, :], wrel_scales[:, h, :], wrel_grp[:, h].rearrange("p c t -> p (c t)"))
+
+        wgr_grp = const.tile([P, 3, 128, 4], BF16, align_bytes=64)
+        wgr_codes = const.tile([P, 3, 128], I32, align_bytes=64)
+        wgr_scales = const.tile([P, 3, 128], U8, align_bytes=64)
+        for h in range(3):
+            d, s = regroup_views(wgr_grp[:, h], wgr_raw[:, 4 * h:4 * h + 4, :])
+            nc.scalar.copy(out=d, in_=s)
+
+        at_ps = []
+        for a in range(2):
+            at_a = atp.tile([P, 4, P], F32, name="at%d" % a)
+            at_ps.append(at_a)
+            for t in range(4):
+                mx(at_a[:, t, :], wrel_codes[:, 0, t * P:(t + 1) * P], wrel_scales[:, 0, t * P:(t + 1) * P],
+                   x_codes[:, a * P:(a + 1) * P], x_scales[:, a * P:(a + 1) * P], True, True)
+        bt_sb = const.tile([P, 256, 4], F32)
+        for a in range(2):
+            bt_ps = hd.tile([P, 4, P], F32, tag="hd")
+            for t in range(4):
+                mx(bt_ps[:, t, :], wrel_codes[:, 1, t * P:(t + 1) * P], wrel_scales[:, 1, t * P:(t + 1) * P],
+                   x_codes[:, a * P:(a + 1) * P], x_scales[:, a * P:(a + 1) * P], True, True)
+            nc.vector.tensor_tensor(
+                out=bt_sb[:, a * P:(a + 1) * P, :],
+                in0=bt_ps[:].rearrange("p t n -> p n t"),
+                in1=bias_sb[:, 0:4].unsqueeze(1).to_broadcast([P, P, 4]),
+                op=ADD,
+            )
+
+        for h in range(3):
+            quantise(wgr_codes[:, h, :], wgr_scales[:, h, :], wgr_grp[:, h].rearrange("p c t -> p (c t)"))
+
+        xj_codes = const.tile([P, 4, 512], I32, align_bytes=64)
+        xj_scales = const.tile([P, 4, 512], U8, align_bytes=64)
+        nc.vector.tensor_copy(
+            out=xj_codes[:].rearrange("p b (i j) -> p b i j", i=8),
+            in_=x_codes[:].rearrange("p (b j) -> p b j", b=4).unsqueeze(2).to_broadcast([P, 4, 8, 64]),
+        )
+        nc.vector.tensor_copy(
+            out=xj_scales[:].rearrange("p b c -> p (b c)").bitcast(I32).rearrange(
+                "p (b i j) -> p b i j", b=4, i=8),
+            in_=x_scales[:].bitcast(I32).rearrange("p (b j) -> p b j", b=4).unsqueeze(2).to_broadcast(
+                [P, 4, 8, 16]),
+        )
+
+        pt_ps = hd.tile([P, 256], F32, tag="hd")
+        mx(pt_ps[:], wgr_codes[:, 0, :], wgr_scales[:, 0, :], x_codes[:], x_scales[:], True, True)
+        ptb_sb = const.tile([P, 256], F32)
+        nc.scalar.activation(out=ptb_sb[:], in_=pt_ps[:], func=ACT.Identity, bias=bias_sb[:, 8:9], scale=1.0)
+
+        rel_bf = {}
+        rel_codes = {}
+        rel_scales = {}
+        th_sb = {}
+
+        def build(g):
+            q, h = divmod(g, 2)
+            b = g // 8
+            c0 = (b % 2) * 64 + (g % 8) * 8
+            if h == 0:
+                rel_bf[q] = relp.tile([P, 4096], BF16, name="rel_bf", tag="rel_bf", align_bytes=64)
+            nc.vector.tensor_tensor(
+                out=rel_bf[q][:, h * 2048:(h + 1) * 2048].rearrange("p (i j t) -> p i j t", i=8, j=64),
+                in0=at_ps[b // 2][:, :, c0:c0 + 8].rearrange("p t i -> p i t").unsqueeze(2).to_broadcast(
+                    [P, 8, 64, 4]),
+                in1=bt_sb[:, b * 64:(b + 1) * 64, :].unsqueeze(1).to_broadcast([P, 8, 64, 4]),
+                op=ADD,
+            )
+
+        def quant_pair(q):
+            rel_codes[q] = relp.tile([P, 1024], I32, name="rel_codes", tag="rel_codes", align_bytes=64)
+            rel_scales[q] = relp.tile([P, 1024], U8, name="rel_scales", tag="rel_scales", align_bytes=64)
+            quantise(rel_codes[q][:], rel_scales[q][:], rel_bf[q][:])
+
+        def product(g):
+            q, h = divmod(g, 2)
+            b = g // 8
+            acc = accp.tile([P, 512], F32, name="acc", tag="acc")
+            mx(acc[:], wgr_codes[:, 1, :], wgr_scales[:, 1, :], xj_codes[:, b, :], xj_scales[:, b, :], True, False)
+            mx(acc[:], wgr_codes[:, 2, :], wgr_scales[:, 2, :],
+               rel_codes[q][:, h * 512:(h + 1) * 512], rel_scales[q][:, h * 512:(h + 1) * 512], False, True)
+            th_sb[g] = thp.tile([P, 512], F32, name="th", tag="th")
+            for i in range(8):
+                tok = g * 8 + i
+                nc.scalar.activation(out=th_sb[g][:, i * 64:(i + 1) * 64], in_=acc[:, i * 64:(i + 1) * 64],
+                                     func=ACT.Tanh, bias=ptb_sb[:, tok:tok + 1], scale=1.0)
+
+        def finish(g):
+            tr = trp.tile([P, 512], F32, name="tr", tag="tr")
+            for k in range(4):
+                nc.tensor.transpose(tr[:, k * P:(k + 1) * P], th_sb[g][:, k * P:(k + 1) * P], ident_f[:])
+            o_sb = outp.tile([P, 4, P], F32, name="o_sb", tag="o_sb")
+            nc.scalar.copy(out=o_sb[:].rearrange("p k f -> p (k f)"), in_=tr[:])
+            nc.sync.dma_start(
+                out=out1_flat[g * 512:(g + 1) * 512, :].rearrange("(k m) f -> m k f", m=P), in_=o_sb[:]
+            )
+
+        def node_update():
+            wgo_grp = const.tile([P, 512, 4], BF16, align_bytes=64)
+            wgo_codes = const.tile([P, 512], I32, align_bytes=64)
+            wgo_scales = const.tile([P, 512], U8, align_bytes=64)
+            d, s = regroup_views(wgo_grp[:], wgo_raw[:])
+            nc.scalar.copy(out=d, in_=s)
+            quantise(wgo_codes[:], wgo_scales[:], wgo_grp[:].rearrange("p c t -> p (c t)"))
+            nxt_sb = const.tile([P, 4, 256], F32)
+            for t in range(4):
+                nx_ps = hd.tile([P, 256], F32, tag="hd")
+                mx(nx_ps[:], wgo_codes[:, t * P:(t + 1) * P], wgo_scales[:, t * P:(t + 1) * P],
+                   x_codes[:], x_scales[:], True, True)
+                nc.scalar.activation(out=nxt_sb[:, t, :], in_=nx_ps[:], func=ACT.Tanh,
+                                     bias=bias_sb[:, 4 + t:5 + t], scale=1.0)
+            for a in range(2):
+                nxr_ps = hd.tile([P, 512], F32, tag="hd")
+                for t in range(4):
+                    nc.tensor.transpose(nxr_ps[:, t * P:(t + 1) * P], nxt_sb[:, t, a * P:(a + 1) * P], ident_f[:])
+                nx_sb = outp.tile([P, 512], F32, name="nx_sb", tag="nx_sb")
+                nc.scalar.copy(out=nx_sb[:], in_=nxr_ps[:])
+                nc.sync.dma_start(out=out0_flat[a * P:(a + 1) * P, :], in_=nx_sb[:])
+
+        NPAIR = 16
+        for q in range(NPAIR + 2):
+            if q < NPAIR:
+                build(2 * q)
+                build(2 * q + 1)
+            if 1 <= q <= NPAIR:
+                quant_pair(q - 1)
+                product(2 * q - 2)
+                product(2 * q - 1)
+            if q >= 2:
+                finish(2 * q - 4)
+                finish(2 * q - 3)
+            if q == 2:
+                node_update()

@@ -14,6 +14,10 @@ ACT = mybir.ActivationFunctionType
 P = 128
 FLOPS = 2 * 256 * 512 * (3 * 512 + 2 * 128) + 2 * 16384 * 512 * 128
 
+MANUAL = True
+CYCLES = [([3 * c, 3 * c + 1], [3 * c + 2]) for c in range(10)] + [([30, 31], [])]
+NODE_AT = 2
+
 
 def tile_languagemsgencoder_pa_t_kernel(
     tc, text_embedding, W_rel, b_rel, W_go, b_go, W_gr, b_gr, out_0, out_1
@@ -44,13 +48,17 @@ def tile_languagemsgencoder_pa_t_kernel(
 
     with ExitStack() as ctx:
         const = ctx.enter_context(tc.tile_pool(name="const", bufs=1))
-        relp = ctx.enter_context(tc.tile_pool(name="relp", bufs=3))
+        relp = ctx.enter_context(tc.tile_pool(name="relp", bufs=4))
+        relg = ctx.enter_context(tc.tile_pool(name="relg", bufs=1))
+        codp = ctx.enter_context(tc.tile_pool(name="codp", bufs=6))
         outp = ctx.enter_context(tc.tile_pool(name="outp", bufs=4))
         thp = ctx.enter_context(tc.tile_pool(name="thp", bufs=6))
         atp = ctx.enter_context(tc.psum_pool(name="atp", bufs=1))
         hd = ctx.enter_context(tc.psum_pool(name="hd", bufs=2))
         accp = ctx.enter_context(tc.psum_pool(name="accp", bufs=2))
         trp = ctx.enter_context(tc.psum_pool(name="trp", bufs=2))
+        if MANUAL:
+            ctx.enter_context(tc.manual_schedule())
 
         x_sb = const.tile([P, 2, 512], BF16)
         wrel_raw = const.tile([P, 8, 512], BF16)
@@ -103,7 +111,8 @@ def tile_languagemsgencoder_pa_t_kernel(
             nc.vector.tensor_copy(out=d, in_=s)
             d, s = regroup_views(wrel_grp[:, h, SPLIT:512, :], wrel_raw[:, 4 * h:4 * h + 4, SPLIT:512])
             nc.scalar.copy(out=d, in_=s)
-        quantise(x_codes[:], x_scales[:], x_grp[:].rearrange("p n t -> p (n t)"))
+            if h == 0:
+                quantise(x_codes[:], x_scales[:], x_grp[:].rearrange("p n t -> p (n t)"))
         for h in range(2):
             quantise(wrel_codes[:, h, :], wrel_scales[:, h, :], wrel_grp[:, h].rearrange("p c t -> p (c t)"))
 
@@ -115,18 +124,31 @@ def tile_languagemsgencoder_pa_t_kernel(
             nc.scalar.copy(out=d, in_=s)
 
         at_ps = []
-        for a in range(2):
+        at_sb = const.tile([P, 256, 4], F32)
+        bt_sb = const.tile([P, 256, 4], F32)
+
+        head_ps = {}
+
+        def first_relation(a):
+            xc, xs = x_codes[:, a * P:(a + 1) * P], x_scales[:, a * P:(a + 1) * P]
             at_a = atp.tile([P, 4, P], F32, name="at%d" % a)
             at_ps.append(at_a)
+            bt_ps = hd.tile([P, 4, P], F32, name="bt_ps", tag="hd")
+            at2_ps = hd.tile([P, 4, P], F32, name="at2_ps", tag="hd")
+            head_ps[a] = (bt_ps, at2_ps)
             for t in range(4):
                 mx(at_a[:, t, :], wrel_codes[:, 0, t * P:(t + 1) * P], wrel_scales[:, 0, t * P:(t + 1) * P],
-                   x_codes[:, a * P:(a + 1) * P], x_scales[:, a * P:(a + 1) * P], True, True)
-        bt_sb = const.tile([P, 256, 4], F32)
-        for a in range(2):
-            bt_ps = hd.tile([P, 4, P], F32, tag="hd")
+                   xc, xs, True, True)
+            for t in range(4):
+                mx(at2_ps[:, t, :], wrel_codes[:, 0, t * P:(t + 1) * P], wrel_scales[:, 0, t * P:(t + 1) * P],
+                   xc, xs, True, True)
             for t in range(4):
                 mx(bt_ps[:, t, :], wrel_codes[:, 1, t * P:(t + 1) * P], wrel_scales[:, 1, t * P:(t + 1) * P],
-                   x_codes[:, a * P:(a + 1) * P], x_scales[:, a * P:(a + 1) * P], True, True)
+                   xc, xs, True, True)
+
+        def first_relation_out(a):
+            bt_ps, at2_ps = head_ps[a]
+            nc.scalar.copy(out=at_sb[:, a * P:(a + 1) * P, :], in_=at2_ps[:].rearrange("p t n -> p n t"))
             nc.vector.tensor_tensor(
                 out=bt_sb[:, a * P:(a + 1) * P, :],
                 in0=bt_ps[:].rearrange("p t n -> p n t"),
@@ -134,58 +156,67 @@ def tile_languagemsgencoder_pa_t_kernel(
                 op=ADD,
             )
 
-        for h in range(3):
-            quantise(wgr_codes[:, h, :], wgr_scales[:, h, :], wgr_grp[:, h].rearrange("p c t -> p (c t)"))
+        first_relation(0)
+        first_relation_out(0)
 
         xj_codes = const.tile([P, 4, 512], I32, align_bytes=64)
         xj_scales = const.tile([P, 4, 512], U8, align_bytes=64)
-        nc.vector.tensor_copy(
-            out=xj_codes[:].rearrange("p b (i j) -> p b i j", i=8),
-            in_=x_codes[:].rearrange("p (b j) -> p b j", b=4).unsqueeze(2).to_broadcast([P, 4, 8, 64]),
-        )
-        nc.vector.tensor_copy(
-            out=xj_scales[:].rearrange("p b c -> p (b c)").bitcast(I32).rearrange(
-                "p (b i j) -> p b i j", b=4, i=8),
-            in_=x_scales[:].bitcast(I32).rearrange("p (b j) -> p b j", b=4).unsqueeze(2).to_broadcast(
-                [P, 4, 8, 16]),
-        )
-
-        pt_ps = hd.tile([P, 256], F32, tag="hd")
-        mx(pt_ps[:], wgr_codes[:, 0, :], wgr_scales[:, 0, :], x_codes[:], x_scales[:], True, True)
         ptb_sb = const.tile([P, 256], F32)
-        nc.scalar.activation(out=ptb_sb[:], in_=pt_ps[:], func=ACT.Identity, bias=bias_sb[:, 8:9], scale=1.0)
+
+        def second_stage_operands():
+            for h in range(3):
+                quantise(wgr_codes[:, h, :], wgr_scales[:, h, :], wgr_grp[:, h].rearrange("p c t -> p (c t)"))
+            nc.vector.tensor_copy(
+                out=xj_codes[:].rearrange("p b (i j) -> p b i j", i=8),
+                in_=x_codes[:].rearrange("p (b j) -> p b j", b=4).unsqueeze(2).to_broadcast([P, 4, 8, 64]),
+            )
+            nc.vector.tensor_copy(
+                out=xj_scales[:].rearrange("p b c -> p (b c)").bitcast(I32).rearrange(
+                    "p (b i j) -> p b i j", b=4, i=8),
+                in_=x_scales[:].bitcast(I32).rearrange("p (b j) -> p b j", b=4).unsqueeze(2).to_broadcast(
+                    [P, 4, 8, 16]),
+            )
+            pt_ps = hd.tile([P, 256], F32, tag="hd")
+            mx(pt_ps[:], wgr_codes[:, 0, :], wgr_scales[:, 0, :], x_codes[:], x_scales[:], True, True)
+            nc.scalar.activation(out=ptb_sb[:], in_=pt_ps[:], func=ACT.Identity, bias=bias_sb[:, 8:9], scale=1.0)
 
         rel_bf = {}
         rel_codes = {}
         rel_scales = {}
         th_sb = {}
 
-        def build(g):
-            q, h = divmod(g, 2)
+        def build(g, on_gpsimd):
             b = g // 8
             c0 = (b % 2) * 64 + (g % 8) * 8
-            if h == 0:
-                rel_bf[q] = relp.tile([P, 4096], BF16, name="rel_bf", tag="rel_bf", align_bytes=64)
-            nc.vector.tensor_tensor(
-                out=rel_bf[q][:, h * 2048:(h + 1) * 2048].rearrange("p (i j t) -> p i j t", i=8, j=64),
-                in0=at_ps[b // 2][:, :, c0:c0 + 8].rearrange("p t i -> p i t").unsqueeze(2).to_broadcast(
-                    [P, 8, 64, 4]),
-                in1=bt_sb[:, b * 64:(b + 1) * 64, :].unsqueeze(1).to_broadcast([P, 8, 64, 4]),
-                op=ADD,
-            )
+            in1 = bt_sb[:, b * 64:(b + 1) * 64, :].unsqueeze(1).to_broadcast([P, 8, 64, 4])
+            if on_gpsimd:
+                rel_bf[g] = relg.tile([P, 2048], BF16, name="rel_g", tag="rel_g", align_bytes=64)
+                nc.gpsimd.tensor_tensor(
+                    out=rel_bf[g][:].rearrange("p (i j t) -> p i j t", i=8, j=64),
+                    in0=at_sb[:, g * 8:g * 8 + 8, :].unsqueeze(2).to_broadcast([P, 8, 64, 4]),
+                    in1=in1,
+                    op=ADD,
+                )
+            else:
+                rel_bf[g] = relp.tile([P, 2048], BF16, name="rel_v", tag="rel_v", align_bytes=64)
+                nc.vector.tensor_tensor(
+                    out=rel_bf[g][:].rearrange("p (i j t) -> p i j t", i=8, j=64),
+                    in0=at_ps[b // 2][:, :, c0:c0 + 8].rearrange("p t i -> p i t").unsqueeze(2).to_broadcast(
+                        [P, 8, 64, 4]),
+                    in1=in1,
+                    op=ADD,
+                )
 
-        def quant_pair(q):
-            rel_codes[q] = relp.tile([P, 1024], I32, name="rel_codes", tag="rel_codes", align_bytes=64)
-            rel_scales[q] = relp.tile([P, 1024], U8, name="rel_scales", tag="rel_scales", align_bytes=64)
-            quantise(rel_codes[q][:], rel_scales[q][:], rel_bf[q][:])
+        def quant(g):
+            rel_codes[g] = codp.tile([P, 512], I32, name="rel_codes", tag="rel_codes", align_bytes=64)
+            rel_scales[g] = codp.tile([P, 512], U8, name="rel_scales", tag="rel_scales", align_bytes=64)
+            quantise(rel_codes[g][:], rel_scales[g][:], rel_bf[g][:])
 
         def product(g):
-            q, h = divmod(g, 2)
             b = g // 8
             acc = accp.tile([P, 512], F32, name="acc", tag="acc")
             mx(acc[:], wgr_codes[:, 1, :], wgr_scales[:, 1, :], xj_codes[:, b, :], xj_scales[:, b, :], True, False)
-            mx(acc[:], wgr_codes[:, 2, :], wgr_scales[:, 2, :],
-               rel_codes[q][:, h * 512:(h + 1) * 512], rel_scales[q][:, h * 512:(h + 1) * 512], False, True)
+            mx(acc[:], wgr_codes[:, 2, :], wgr_scales[:, 2, :], rel_codes[g][:], rel_scales[g][:], False, True)
             th_sb[g] = thp.tile([P, 512], F32, name="th", tag="th")
             for i in range(8):
                 tok = g * 8 + i
@@ -202,39 +233,50 @@ def tile_languagemsgencoder_pa_t_kernel(
                 out=out1_flat[g * 512:(g + 1) * 512, :].rearrange("(k m) f -> m k f", m=P), in_=o_sb[:]
             )
 
+        wgo_grp = const.tile([P, 512, 4], BF16, align_bytes=64)
+        wgo_codes = const.tile([P, 512], I32, align_bytes=64)
+        wgo_scales = const.tile([P, 512], U8, align_bytes=64)
+        nxt_sb = const.tile([P, 4, 256], F32)
+
         def node_update():
-            wgo_grp = const.tile([P, 512, 4], BF16, align_bytes=64)
-            wgo_codes = const.tile([P, 512], I32, align_bytes=64)
-            wgo_scales = const.tile([P, 512], U8, align_bytes=64)
-            d, s = regroup_views(wgo_grp[:], wgo_raw[:])
-            nc.scalar.copy(out=d, in_=s)
-            quantise(wgo_codes[:], wgo_scales[:], wgo_grp[:].rearrange("p c t -> p (c t)"))
-            nxt_sb = const.tile([P, 4, 256], F32)
             for t in range(4):
-                nx_ps = hd.tile([P, 256], F32, tag="hd")
+                nx_ps = hd.tile([P, 256], F32, name="nx_ps", tag="hd")
                 mx(nx_ps[:], wgo_codes[:, t * P:(t + 1) * P], wgo_scales[:, t * P:(t + 1) * P],
                    x_codes[:], x_scales[:], True, True)
                 nc.scalar.activation(out=nxt_sb[:, t, :], in_=nx_ps[:], func=ACT.Tanh,
                                      bias=bias_sb[:, 4 + t:5 + t], scale=1.0)
             for a in range(2):
-                nxr_ps = hd.tile([P, 512], F32, tag="hd")
+                nxr_ps = hd.tile([P, 512], F32, name="nxr_ps", tag="hd")
                 for t in range(4):
                     nc.tensor.transpose(nxr_ps[:, t * P:(t + 1) * P], nxt_sb[:, t, a * P:(a + 1) * P], ident_f[:])
                 nx_sb = outp.tile([P, 512], F32, name="nx_sb", tag="nx_sb")
                 nc.scalar.copy(out=nx_sb[:], in_=nxr_ps[:])
                 nc.sync.dma_start(out=out0_flat[a * P:(a + 1) * P, :], in_=nx_sb[:])
 
-        NPAIR = 16
-        for q in range(NPAIR + 2):
-            if q < NPAIR:
-                build(2 * q)
-                build(2 * q + 1)
-            if 1 <= q <= NPAIR:
-                quant_pair(q - 1)
-                product(2 * q - 2)
-                product(2 * q - 1)
-            if q >= 2:
-                finish(2 * q - 4)
-                finish(2 * q - 3)
-            if q == 2:
+        previous = []
+        for c, (v_groups, g_groups) in enumerate(CYCLES):
+            for g in g_groups:
+                build(g, True)
+            for g in v_groups:
+                build(g, False)
+            if c == 0:
+                second_stage_operands()
+                first_relation(1)
+            if c == 1:
+                first_relation_out(1)
+            if c == NODE_AT - 1:
+                d, s = regroup_views(wgo_grp[:], wgo_raw[:])
+                nc.scalar.copy(out=d, in_=s)
+            for g in previous:
+                finish(g)
+            if c == NODE_AT:
+                quantise(wgo_codes[:], wgo_scales[:], wgo_grp[:].rearrange("p c t -> p (c t)"))
+            for g in v_groups + g_groups:
+                quant(g)
+            for g in v_groups + g_groups:
+                product(g)
+            if c == NODE_AT:
                 node_update()
+            previous = v_groups + g_groups
+        for g in previous:
+            finish(g)

@@ -15,7 +15,24 @@ P = 128
 FLOPS = 2 * 256 * 512 * (3 * 512 + 2 * 128) + 2 * 16384 * 512 * 128
 
 MANUAL = True
-CYCLES = [([3 * c, 3 * c + 1], [3 * c + 2]) for c in range(10)] + [([30, 31], [])]
+S_PATH = False
+
+
+def schedule():
+    cycles = []
+    if S_PATH:
+        for k in range(3):
+            base = 80 * k
+            su = (base + 72, 8)
+            cycles.append(([(base, 8), (base + 8, 8)], [(base + 16, 8)], [], (su, 0, 3)))
+            cycles.append(([(base + 24, 8), (base + 32, 8)], [(base + 40, 8)], [], (su, 3, 6)))
+            cycles.append(([(base + 48, 8), (base + 56, 8)], [(base + 64, 8)], [su], (su, 6, 8)))
+    else:
+        for c in range(10):
+            cycles.append(([(24 * c, 8), (24 * c + 8, 8)], [(24 * c + 16, 8)], [], None))
+    cycles.append(([(240, 8)], [(248, 4)], [], None))
+    cycles.append(([(252, 4)], [], [], None))
+    return cycles
 NODE_AT = 2
 
 
@@ -50,9 +67,10 @@ def tile_languagemsgencoder_pa_t_kernel(
         const = ctx.enter_context(tc.tile_pool(name="const", bufs=1))
         relp = ctx.enter_context(tc.tile_pool(name="relp", bufs=4))
         relg = ctx.enter_context(tc.tile_pool(name="relg", bufs=1))
-        codp = ctx.enter_context(tc.tile_pool(name="codp", bufs=6))
+        rels = ctx.enter_context(tc.tile_pool(name="rels", bufs=1))
+        codp = ctx.enter_context(tc.tile_pool(name="codp", bufs=8))
         outp = ctx.enter_context(tc.tile_pool(name="outp", bufs=4))
-        thp = ctx.enter_context(tc.tile_pool(name="thp", bufs=6))
+        thp = ctx.enter_context(tc.tile_pool(name="thp", bufs=8))
         atp = ctx.enter_context(tc.psum_pool(name="atp", bufs=1))
         hd = ctx.enter_context(tc.psum_pool(name="hd", bufs=2))
         accp = ctx.enter_context(tc.psum_pool(name="accp", bufs=2))
@@ -100,30 +118,27 @@ def tile_languagemsgencoder_pa_t_kernel(
         b_ps = hd.tile([P, P], BF16, tag="hd")
         nc.tensor.transpose(b_ps[:], bias_rows[:], ident_bf[:])
         bias_sb = const.tile([P, 16], F32)
-        nc.scalar.copy(out=bias_sb[:], in_=b_ps[:, 0:16])
 
         wrel_grp = const.tile([P, 2, 512, 4], BF16, align_bytes=64)
         wrel_codes = const.tile([P, 2, 512], I32, align_bytes=64)
         wrel_scales = const.tile([P, 2, 512], U8, align_bytes=64)
-        SPLIT = 320
+        SPLITS = (128, 192)
         for h in range(2):
-            d, s = regroup_views(wrel_grp[:, h, 0:SPLIT, :], wrel_raw[:, 4 * h:4 * h + 4, 0:SPLIT])
-            nc.vector.tensor_copy(out=d, in_=s)
-            d, s = regroup_views(wrel_grp[:, h, SPLIT:512, :], wrel_raw[:, 4 * h:4 * h + 4, SPLIT:512])
+            d, s = regroup_views(wrel_grp[:, h, 0:SPLITS[h], :], wrel_raw[:, 4 * h:4 * h + 4, 0:SPLITS[h]])
             nc.scalar.copy(out=d, in_=s)
             if h == 0:
+                nc.scalar.copy(out=bias_sb[:], in_=b_ps[:, 0:16])
+            d, s = regroup_views(wrel_grp[:, h, SPLITS[h]:512, :], wrel_raw[:, 4 * h:4 * h + 4, SPLITS[h]:512])
+            nc.vector.tensor_copy(out=d, in_=s)
+            if h == 0:
                 quantise(x_codes[:], x_scales[:], x_grp[:].rearrange("p n t -> p (n t)"))
-        for h in range(2):
             quantise(wrel_codes[:, h, :], wrel_scales[:, h, :], wrel_grp[:, h].rearrange("p c t -> p (c t)"))
 
         wgr_grp = const.tile([P, 3, 128, 4], BF16, align_bytes=64)
         wgr_codes = const.tile([P, 3, 128], I32, align_bytes=64)
         wgr_scales = const.tile([P, 3, 128], U8, align_bytes=64)
-        for h in range(3):
-            d, s = regroup_views(wgr_grp[:, h], wgr_raw[:, 4 * h:4 * h + 4, :])
-            nc.scalar.copy(out=d, in_=s)
 
-        at_ps = []
+        bt_ps = []
         at_sb = const.tile([P, 256, 4], F32)
         bt_sb = const.tile([P, 256, 4], F32)
 
@@ -131,51 +146,49 @@ def tile_languagemsgencoder_pa_t_kernel(
 
         def first_relation(a):
             xc, xs = x_codes[:, a * P:(a + 1) * P], x_scales[:, a * P:(a + 1) * P]
-            at_a = atp.tile([P, 4, P], F32, name="at%d" % a)
-            at_ps.append(at_a)
-            bt_ps = hd.tile([P, 4, P], F32, name="bt_ps", tag="hd")
-            at2_ps = hd.tile([P, 4, P], F32, name="at2_ps", tag="hd")
-            head_ps[a] = (bt_ps, at2_ps)
-            for t in range(4):
-                mx(at_a[:, t, :], wrel_codes[:, 0, t * P:(t + 1) * P], wrel_scales[:, 0, t * P:(t + 1) * P],
-                   xc, xs, True, True)
-            for t in range(4):
-                mx(at2_ps[:, t, :], wrel_codes[:, 0, t * P:(t + 1) * P], wrel_scales[:, 0, t * P:(t + 1) * P],
-                   xc, xs, True, True)
-            for t in range(4):
-                mx(bt_ps[:, t, :], wrel_codes[:, 1, t * P:(t + 1) * P], wrel_scales[:, 1, t * P:(t + 1) * P],
-                   xc, xs, True, True)
+            bt_a = atp.tile([P, 4, P], F32, name="bt%d" % a)
+            bt_ps.append(bt_a)
+            at_tmp = hd.tile([P, 4, P], F32, name="at_tmp", tag="hd")
+            bt_tmp = hd.tile([P, 4, P], F32, name="bt_tmp", tag="hd")
+            head_ps[a] = (at_tmp, bt_tmp)
+            for dst, h in ((at_tmp, 0), (bt_a, 1), (bt_tmp, 1)):
+                for t in range(4):
+                    mx(dst[:, t, :], wrel_codes[:, h, t * P:(t + 1) * P], wrel_scales[:, h, t * P:(t + 1) * P],
+                       xc, xs, True, True)
 
         def first_relation_out(a):
-            bt_ps, at2_ps = head_ps[a]
-            nc.scalar.copy(out=at_sb[:, a * P:(a + 1) * P, :], in_=at2_ps[:].rearrange("p t n -> p n t"))
+            at_tmp, bt_tmp = head_ps[a]
             nc.vector.tensor_tensor(
-                out=bt_sb[:, a * P:(a + 1) * P, :],
-                in0=bt_ps[:].rearrange("p t n -> p n t"),
+                out=at_sb[:, a * P:(a + 1) * P, :],
+                in0=at_tmp[:].rearrange("p t n -> p n t"),
                 in1=bias_sb[:, 0:4].unsqueeze(1).to_broadcast([P, P, 4]),
                 op=ADD,
             )
+            nc.scalar.copy(out=bt_sb[:, a * P:(a + 1) * P, :], in_=bt_tmp[:].rearrange("p t n -> p n t"))
 
         first_relation(0)
         first_relation_out(0)
 
-        xj_codes = const.tile([P, 4, 512], I32, align_bytes=64)
-        xj_scales = const.tile([P, 4, 512], U8, align_bytes=64)
+        xj_codes = const.tile([P, 4, 256], I32, align_bytes=64)
+        xj_scales = const.tile([P, 4, 256], U8, align_bytes=64)
+        nc.vector.tensor_copy(
+            out=xj_codes[:].rearrange("p b (i j) -> p b i j", i=4),
+            in_=x_codes[:].rearrange("p (b j) -> p b j", b=4).unsqueeze(2).to_broadcast([P, 4, 4, 64]),
+        )
+        for h in range(3):
+            d, s = regroup_views(wgr_grp[:, h], wgr_raw[:, 4 * h:4 * h + 4, :])
+            nc.scalar.copy(out=d, in_=s)
         ptb_sb = const.tile([P, 256], F32)
 
         def second_stage_operands():
-            for h in range(3):
-                quantise(wgr_codes[:, h, :], wgr_scales[:, h, :], wgr_grp[:, h].rearrange("p c t -> p (c t)"))
-            nc.vector.tensor_copy(
-                out=xj_codes[:].rearrange("p b (i j) -> p b i j", i=8),
-                in_=x_codes[:].rearrange("p (b j) -> p b j", b=4).unsqueeze(2).to_broadcast([P, 4, 8, 64]),
-            )
             nc.vector.tensor_copy(
                 out=xj_scales[:].rearrange("p b c -> p (b c)").bitcast(I32).rearrange(
-                    "p (b i j) -> p b i j", b=4, i=8),
+                    "p (b i j) -> p b i j", b=4, i=4),
                 in_=x_scales[:].bitcast(I32).rearrange("p (b j) -> p b j", b=4).unsqueeze(2).to_broadcast(
-                    [P, 4, 8, 16]),
+                    [P, 4, 4, 16]),
             )
+            for h in range(3):
+                quantise(wgr_codes[:, h, :], wgr_scales[:, h, :], wgr_grp[:, h].rearrange("p c t -> p (c t)"))
             pt_ps = hd.tile([P, 256], F32, tag="hd")
             mx(pt_ps[:], wgr_codes[:, 0, :], wgr_scales[:, 0, :], x_codes[:], x_scales[:], True, True)
             nc.scalar.activation(out=ptb_sb[:], in_=pt_ps[:], func=ACT.Identity, bias=bias_sb[:, 8:9], scale=1.0)
@@ -185,52 +198,88 @@ def tile_languagemsgencoder_pa_t_kernel(
         rel_scales = {}
         th_sb = {}
 
-        def build(g, on_gpsimd):
-            b = g // 8
-            c0 = (b % 2) * 64 + (g % 8) * 8
-            in1 = bt_sb[:, b * 64:(b + 1) * 64, :].unsqueeze(1).to_broadcast([P, 8, 64, 4])
+        def build(u, on_gpsimd):
+            tok0, n = u
+            b = tok0 // 64
+            c0 = (b % 2) * 64
+            in0 = at_sb[:, tok0:tok0 + n, :].unsqueeze(2).to_broadcast([P, n, 64, 4])
             if on_gpsimd:
-                rel_bf[g] = relg.tile([P, 2048], BF16, name="rel_g", tag="rel_g", align_bytes=64)
+                rel_bf[u] = relg.tile([P, n * 256], BF16, name="rel_g", tag="rel_g", align_bytes=64)
                 nc.gpsimd.tensor_tensor(
-                    out=rel_bf[g][:].rearrange("p (i j t) -> p i j t", i=8, j=64),
-                    in0=at_sb[:, g * 8:g * 8 + 8, :].unsqueeze(2).to_broadcast([P, 8, 64, 4]),
-                    in1=in1,
+                    out=rel_bf[u][:].rearrange("p (i j t) -> p i j t", i=n, j=64),
+                    in0=in0,
+                    in1=bt_sb[:, b * 64:(b + 1) * 64, :].unsqueeze(1).to_broadcast([P, n, 64, 4]),
                     op=ADD,
                 )
             else:
-                rel_bf[g] = relp.tile([P, 2048], BF16, name="rel_v", tag="rel_v", align_bytes=64)
+                rel_bf[u] = relp.tile([P, n * 256], BF16, name="rel_v", tag="rel_v", align_bytes=64)
                 nc.vector.tensor_tensor(
-                    out=rel_bf[g][:].rearrange("p (i j t) -> p i j t", i=8, j=64),
-                    in0=at_ps[b // 2][:, :, c0:c0 + 8].rearrange("p t i -> p i t").unsqueeze(2).to_broadcast(
-                        [P, 8, 64, 4]),
-                    in1=in1,
+                    out=rel_bf[u][:].rearrange("p (i j t) -> p i j t", i=n, j=64),
+                    in0=in0,
+                    in1=bt_ps[b // 2][:, :, c0:c0 + 64].rearrange("p t j -> p j t").unsqueeze(1).to_broadcast(
+                        [P, n, 64, 4]),
                     op=ADD,
                 )
 
-        def quant(g):
-            rel_codes[g] = codp.tile([P, 512], I32, name="rel_codes", tag="rel_codes", align_bytes=64)
-            rel_scales[g] = codp.tile([P, 512], U8, name="rel_scales", tag="rel_scales", align_bytes=64)
-            quantise(rel_codes[g][:], rel_scales[g][:], rel_bf[g][:])
+        planes = {}
 
-        def product(g):
-            b = g // 8
-            acc = accp.tile([P, 512], F32, name="acc", tag="acc")
-            mx(acc[:], wgr_codes[:, 1, :], wgr_scales[:, 1, :], xj_codes[:, b, :], xj_scales[:, b, :], True, False)
-            mx(acc[:], wgr_codes[:, 2, :], wgr_scales[:, 2, :], rel_codes[g][:], rel_scales[g][:], False, True)
-            th_sb[g] = thp.tile([P, 512], F32, name="th", tag="th")
-            for i in range(8):
-                tok = g * 8 + i
-                nc.scalar.activation(out=th_sb[g][:, i * 64:(i + 1) * 64], in_=acc[:, i * 64:(i + 1) * 64],
+        def build_on_scalar(u, i_lo, i_hi):
+            tok0, n = u
+            b = tok0 // 64
+            if i_lo == 0:
+                planes[u] = rels.tile([P, 4, n * 64], BF16, name="planes", tag="planes")
+                rel_bf[u] = rels.tile([P, n * 256], BF16, name="rel_s", tag="rel_s", align_bytes=64)
+            for i in range(i_lo, i_hi):
+                for t in range(4):
+                    nc.scalar.activation(out=planes[u][:, t, i * 64:(i + 1) * 64],
+                                         in_=bt_sb[:, b * 64:(b + 1) * 64, t], func=ACT.Identity,
+                                         bias=at_sb[:, tok0 + i, t:t + 1], scale=1.0)
+            d, s = regroup_views(
+                rel_bf[u][:].rearrange("p (w t) -> p w t", t=4)[:, i_lo * 64:i_hi * 64, :],
+                planes[u][:, :, i_lo * 64:i_hi * 64],
+            )
+            nc.scalar.copy(out=d, in_=s)
+
+        def quant(u):
+            n = u[1]
+            rel_codes[u] = codp.tile([P, n * 64], I32, name="rel_codes", tag="rel_codes", align_bytes=64)
+            rel_scales[u] = codp.tile([P, n * 64], U8, name="rel_scales", tag="rel_scales", align_bytes=64)
+            quantise(rel_codes[u][:], rel_scales[u][:], rel_bf[u][:])
+
+        def product(u):
+            tok0, n = u
+            b = tok0 // 64
+            acc = accp.tile([P, n * 64], F32, name="acc", tag="acc")
+            for hf in range(n // 4):
+                cols = slice(hf * 256, (hf + 1) * 256)
+                mx(acc[:, cols], wgr_codes[:, 1, :], wgr_scales[:, 1, :], xj_codes[:, b, :], xj_scales[:, b, :],
+                   True, False)
+                mx(acc[:, cols], wgr_codes[:, 2, :], wgr_scales[:, 2, :], rel_codes[u][:, cols],
+                   rel_scales[u][:, cols], False, True)
+            th_sb[u] = thp.tile([P, n * 64], F32, name="th", tag="th")
+            for i in range(n):
+                tok = tok0 + i
+                nc.scalar.activation(out=th_sb[u][:, i * 64:(i + 1) * 64], in_=acc[:, i * 64:(i + 1) * 64],
                                      func=ACT.Tanh, bias=ptb_sb[:, tok:tok + 1], scale=1.0)
 
-        def finish(g):
-            tr = trp.tile([P, 512], F32, name="tr", tag="tr")
-            for k in range(4):
-                nc.tensor.transpose(tr[:, k * P:(k + 1) * P], th_sb[g][:, k * P:(k + 1) * P], ident_f[:])
-            o_sb = outp.tile([P, 4, P], F32, name="o_sb", tag="o_sb")
-            nc.scalar.copy(out=o_sb[:].rearrange("p k f -> p (k f)"), in_=tr[:])
+        tr_ps = {}
+
+        def turn(u):
+            n = u[1]
+            tr_ps[u] = trp.tile([P, n * 64], F32, name="tr", tag="tr")
+            for k in range(n // 2):
+                nc.tensor.transpose(tr_ps[u][:, k * P:(k + 1) * P], th_sb[u][:, k * P:(k + 1) * P], ident_f[:])
+
+        def store(u, on_vector):
+            tok0, n = u
+            tr = tr_ps[u]
+            o_sb = outp.tile([P, n // 2, P], F32, name="o_sb", tag="o_sb")
+            if on_vector:
+                nc.vector.tensor_copy(out=o_sb[:].rearrange("p k f -> p (k f)"), in_=tr[:])
+            else:
+                nc.scalar.copy(out=o_sb[:].rearrange("p k f -> p (k f)"), in_=tr[:])
             nc.sync.dma_start(
-                out=out1_flat[g * 512:(g + 1) * 512, :].rearrange("(k m) f -> m k f", m=P), in_=o_sb[:]
+                out=out1_flat[tok0 * 64:(tok0 + n) * 64, :].rearrange("(k m) f -> m k f", m=P), in_=o_sb[:]
             )
 
         wgo_grp = const.tile([P, 512, 4], BF16, align_bytes=64)
@@ -254,29 +303,38 @@ def tile_languagemsgencoder_pa_t_kernel(
                 nc.sync.dma_start(out=out0_flat[a * P:(a + 1) * P, :], in_=nx_sb[:])
 
         previous = []
-        for c, (v_groups, g_groups) in enumerate(CYCLES):
-            for g in g_groups:
-                build(g, True)
-            for g in v_groups:
-                build(g, False)
-            if c == 0:
-                second_stage_operands()
-                first_relation(1)
+        cycles = schedule()
+        last = len(cycles) - 1
+        for c, (v_units, g_units, s_units, s_part) in enumerate(cycles):
+            units = v_units + s_units + g_units
+            for u in g_units:
+                build(u, True)
+            for u in v_units:
+                build(u, False)
             if c == 1:
                 first_relation_out(1)
-            if c == NODE_AT - 1:
+            for u in previous:
+                turn(u)
+                if c < last:
+                    store(u, False)
+            if s_part is not None:
+                build_on_scalar(s_part[0], s_part[1], s_part[2])
+            if c == 0:
                 d, s = regroup_views(wgo_grp[:], wgo_raw[:])
                 nc.scalar.copy(out=d, in_=s)
-            for g in previous:
-                finish(g)
+                second_stage_operands()
+                first_relation(1)
             if c == NODE_AT:
                 quantise(wgo_codes[:], wgo_scales[:], wgo_grp[:].rearrange("p c t -> p (c t)"))
-            for g in v_groups + g_groups:
-                quant(g)
-            for g in v_groups + g_groups:
-                product(g)
+            for u in units:
+                quant(u)
+            for u in units:
+                product(u)
+            if c == last:
+                for u in previous:
+                    store(u, True)
+                turn(units[0])
+                store(units[0], True)
             if c == NODE_AT:
                 node_update()
-            previous = v_groups + g_groups
-        for g in previous:
-            finish(g)
+            previous = units

@@ -65,8 +65,7 @@ def tile_languagemsgencoder_pa_t_kernel(
 
     with ExitStack() as ctx:
         const = ctx.enter_context(tc.tile_pool(name="const", bufs=1))
-        relp = ctx.enter_context(tc.tile_pool(name="relp", bufs=4))
-        relg = ctx.enter_context(tc.tile_pool(name="relg", bufs=1))
+        relp = ctx.enter_context(tc.tile_pool(name="relp", bufs=1))
         rels = ctx.enter_context(tc.tile_pool(name="rels", bufs=1))
         codp = ctx.enter_context(tc.tile_pool(name="codp", bufs=8))
         outp = ctx.enter_context(tc.tile_pool(name="outp", bufs=4))
@@ -198,13 +197,13 @@ def tile_languagemsgencoder_pa_t_kernel(
         rel_scales = {}
         th_sb = {}
 
-        def build(u, on_gpsimd):
+        def build(u, on_gpsimd, slot):
             tok0, n = u
             b = tok0 // 64
             c0 = (b % 2) * 64
             in0 = at_sb[:, tok0:tok0 + n, :].unsqueeze(2).to_broadcast([P, n, 64, 4])
             if on_gpsimd:
-                rel_bf[u] = relg.tile([P, n * 256], BF16, name="rel_g", tag="rel_g", align_bytes=64)
+                rel_bf[u] = relp.tile([P, n * 256], BF16, name="rel_g", tag=slot, align_bytes=64)
                 nc.gpsimd.tensor_tensor(
                     out=rel_bf[u][:].rearrange("p (i j t) -> p i j t", i=n, j=64),
                     in0=in0,
@@ -212,7 +211,7 @@ def tile_languagemsgencoder_pa_t_kernel(
                     op=ADD,
                 )
             else:
-                rel_bf[u] = relp.tile([P, n * 256], BF16, name="rel_v", tag="rel_v", align_bytes=64)
+                rel_bf[u] = relp.tile([P, n * 256], BF16, name="rel_v", tag=slot, align_bytes=64)
                 nc.vector.tensor_tensor(
                     out=rel_bf[u][:].rearrange("p (i j t) -> p i j t", i=n, j=64),
                     in0=in0,
@@ -307,10 +306,11 @@ def tile_languagemsgencoder_pa_t_kernel(
         last = len(cycles) - 1
         for c, (v_units, g_units, s_units, s_part) in enumerate(cycles):
             units = v_units + s_units + g_units
+            slot_g, slot_v2 = ("relZ", "relY") if c % 2 == 0 else ("relY", "relZ")
             for u in g_units:
-                build(u, True)
-            for u in v_units:
-                build(u, False)
+                build(u, True, slot_g)
+            for u, slot in zip(v_units, ("relX", slot_v2)):
+                build(u, False, slot)
             if c == 1:
                 first_relation_out(1)
             for u in previous:

@@ -165,6 +165,13 @@ def tile_languagemsgencoder_pa_t_kernel(
             )
             nc.scalar.copy(out=bt_sb[:, a * P:(a + 1) * P, :], in_=bt_tmp[:].rearrange("p t n -> p n t"))
 
+        wgo_grp = const.tile([P, 512, 4], BF16, align_bytes=64)
+        for h in range(3):
+            d, s = regroup_views(wgr_grp[:, h], wgr_raw[:, 4 * h:4 * h + 4, :])
+            nc.scalar.copy(out=d, in_=s)
+        d, s = regroup_views(wgo_grp[:], wgo_raw[:])
+        nc.scalar.copy(out=d, in_=s)
+
         first_relation(0)
         first_relation_out(0)
 
@@ -174,9 +181,7 @@ def tile_languagemsgencoder_pa_t_kernel(
             out=xj_codes[:].rearrange("p b (i j) -> p b i j", i=4),
             in_=x_codes[:].rearrange("p (b j) -> p b j", b=4).unsqueeze(2).to_broadcast([P, 4, 4, 64]),
         )
-        for h in range(3):
-            d, s = regroup_views(wgr_grp[:, h], wgr_raw[:, 4 * h:4 * h + 4, :])
-            nc.scalar.copy(out=d, in_=s)
+        first_relation(1)
         ptb_sb = const.tile([P, 256], F32)
 
         def second_stage_operands():
@@ -281,7 +286,6 @@ def tile_languagemsgencoder_pa_t_kernel(
                 out=out1_flat[tok0 * 64:(tok0 + n) * 64, :].rearrange("(k m) f -> m k f", m=P), in_=o_sb[:]
             )
 
-        wgo_grp = const.tile([P, 512, 4], BF16, align_bytes=64)
         wgo_codes = const.tile([P, 512], I32, align_bytes=64)
         wgo_scales = const.tile([P, 512], U8, align_bytes=64)
         nxt_sb = const.tile([P, 4, 256], F32)
@@ -311,21 +315,16 @@ def tile_languagemsgencoder_pa_t_kernel(
                 build(u, True, slot_g)
             for u, slot in zip(v_units, ("relX", slot_v2)):
                 build(u, False, slot)
-            if c == 1:
+            if c == 0:
                 first_relation_out(1)
+                second_stage_operands()
+                quantise(wgo_codes[:], wgo_scales[:], wgo_grp[:].rearrange("p c t -> p (c t)"))
             for u in previous:
                 turn(u)
                 if c < last:
                     store(u, False)
             if s_part is not None:
                 build_on_scalar(s_part[0], s_part[1], s_part[2])
-            if c == 0:
-                d, s = regroup_views(wgo_grp[:], wgo_raw[:])
-                nc.scalar.copy(out=d, in_=s)
-                second_stage_operands()
-                first_relation(1)
-            if c == NODE_AT:
-                quantise(wgo_codes[:], wgo_scales[:], wgo_grp[:].rearrange("p c t -> p (c t)"))
             for u in units:
                 quant(u)
             for u in units:

@@ -169,11 +169,11 @@ def tile_languagemsgencoder_pa_t_kernel(
         for h in range(3):
             d, s = regroup_views(wgr_grp[:, h], wgr_raw[:, 4 * h:4 * h + 4, :])
             nc.scalar.copy(out=d, in_=s)
-        d, s = regroup_views(wgo_grp[:], wgo_raw[:])
-        nc.scalar.copy(out=d, in_=s)
 
         first_relation(0)
         first_relation_out(0)
+        d, s = regroup_views(wgo_grp[:], wgo_raw[:])
+        nc.scalar.copy(out=d, in_=s)
 
         xj_codes = const.tile([P, 4, 256], I32, align_bytes=64)
         xj_scales = const.tile([P, 4, 256], U8, align_bytes=64)

from contextlib import ExitStack

import concourse.mybir as mybir
from concourse.masks import make_identity

F32 = mybir.dt.float32
BF16 = mybir.dt.bfloat16
I32 = mybir.dt.int32
U8 = mybir.dt.uint8
FP8X4 = mybir.dt.float8_e4m3fn_x4
ADD = mybir.AluOpType.add
ACT = mybir.ActivationFunctionType

P = 128
FLOPS = 2 * 256 * 512 * (3 * 512 + 2 * 128) + 2 * 16384 * 512 * 128

MANUAL = True
S_PATH = False


def schedule():
    cycles = []
    if S_PATH:
        for k in range(3):
            base = 80 * k
            su = (base + 72, 8)
            cycles.append(([(base, 8), (base + 8, 8)], [(base + 16, 8)], [], (su, 0, 3)))
            cycles.append(([(base + 24, 8), (base + 32, 8)], [(base + 40, 8)], [], (su, 3, 6)))
            cycles.append(([(base + 48, 8), (base + 56, 8)], [(base + 64, 8)], [su], (su, 6, 8)))
    else:
        for c in range(10):
            cycles.append(([(24 * c, 8), (24 * c + 8, 8)], [(24 * c + 16, 8)], [], None))
    cycles.append(([(240, 8)], [(248, 4)], [], None))
    cycles.append(([(252, 4)], [], [], None))
    return cycles
NODE_AT = 2


def tile_languagemsgencoder_pa_t_kernel(
    tc, text_embedding, W_rel, b_rel, W_go, b_go, W_gr, b_gr, out_0, out_1
):
    nc = tc.nc
    out0_flat = out_0.rearrange("b n d -> (b n) d")
    out1_flat = out_1.rearrange("b i j f -> (b i j) f")

    def mx(out, l_codes, l_scales, r_codes, r_scales, start, stop):
        nc.tensor.matmul_mx(
            out=out,
            lhsT=l_codes.bitcast(FP8X4),
            lhsT_scale=l_scales,
            rhs=r_codes.bitcast(FP8X4),
            rhs_scale=r_scales,
            start=start,
            stop=stop,
        )

    def quantise(codes, scales, grouped):
        nc.vector.quantize_mx(out=codes.bitcast(FP8X4), scales=scales, in_=grouped)

    def regroup_views(dst, src):
        return (
            dst.rearrange("p (c i) t -> p c t i", i=4),
            src.rearrange("p t (c i) -> p c t i", i=4),
        )

    with ExitStack() as ctx:
        const = ctx.enter_context(tc.tile_pool(name="const", bufs=1))
        relp = ctx.enter_context(tc.tile_pool(name="relp", bufs=1))
        rels = ctx.enter_context(tc.tile_pool(name="rels", bufs=1))
        codp = ctx.enter_context(tc.tile_pool(name="codp", bufs=8))
        outp = ctx.enter_context(tc.tile_pool(name="outp", bufs=4))
        thp = ctx.enter_context(tc.tile_pool(name="thp", bufs=8))
        atp = ctx.enter_context(tc.psum_pool(name="atp", bufs=1))
        hd = ctx.enter_context(tc.psum_pool(name="hd", bufs=2))
        accp = ctx.enter_context(tc.psum_pool(name="accp", bufs=2))
        trp = ctx.enter_context(tc.psum_pool(name="trp", bufs=2))
        if MANUAL:
            ctx.enter_context(tc.manual_schedule())

        x_sb = const.tile([P, 2, 512], BF16)
        wrel_raw = const.tile([P, 8, 512], BF16)
        wgr_raw = const.tile([P, 12, 128], BF16)
        wgo_raw = const.tile([P, 4, 512], BF16)
        bias_rows = const.tile([P, P], BF16)
        x_scales = const.tile([P, 256], U8, align_bytes=64)

        nc.vector.memset(bias_rows[:], 0.0)
        nc.vector.memset(x_scales[:].bitcast(I32), 0)

        nc.sync.dma_start(
            out=x_sb[:],
            in_=text_embedding.rearrange("b n d -> (b n) d").rearrange("(a p) d -> p a d", p=P),
        )
        nc.sync.dma_start(out=wrel_raw[:, 0:4, :], in_=W_rel[0:512, :].rearrange("(t p) c -> p t c", p=P))
        nc.sync.dma_start(out=wrel_raw[:, 4:8, :], in_=W_rel[512:1024, :].rearrange("(t p) c -> p t c", p=P))
        nc.scalar.dma_start(out=bias_rows[0:4, :], in_=b_rel.rearrange("(t p) -> t p", p=P))
        nc.scalar.dma_start(out=bias_rows[4:8, :], in_=b_go.rearrange("(t p) -> t p", p=P))
        nc.scalar.dma_start(out=bias_rows[8:9, :], in_=b_gr.rearrange("(o p) -> o p", o=1))
        nc.sync.dma_start(out=wgr_raw[:], in_=W_gr.rearrange("(h p) c -> p h c", p=P))
        nc.sync.dma_start(out=wgo_raw[:], in_=W_go.rearrange("(t p) c -> p t c", p=P))

        ident_bf = const.tile([P, P], BF16)
        make_identity(nc, ident_bf[:])
        ident_f = const.tile([P, P], F32)
        make_identity(nc, ident_f[:])

        xt_ps = hd.tile([P, 4, 256], BF16, tag="hd")
        for a in range(2):
            for t in range(4):
                nc.tensor.transpose(
                    xt_ps[:, t, a * P:(a + 1) * P], x_sb[:, a, t * P:(t + 1) * P], ident_bf[:]
                )
        x_grp = const.tile([P, 256, 4], BF16, align_bytes=64)
        x_codes = const.tile([P, 256], I32, align_bytes=64)
        nc.vector.tensor_copy(out=x_grp[:], in_=xt_ps[:].rearrange("p t n -> p n t"))

        b_ps = hd.tile([P, P], BF16, tag="hd")
        nc.tensor.transpose(b_ps[:], bias_rows[:], ident_bf[:])
        bias_sb = const.tile([P, 16], F32)

        wrel_grp = const.tile([P, 2, 512, 4], BF16, align_bytes=64)
        wrel_codes = const.tile([P, 2, 512], I32, align_bytes=64)
        wrel_scales = const.tile([P, 2, 512], U8, align_bytes=64)
        SPLITS = (128, 192)
        for h in range(2):
            d, s = regroup_views(wrel_grp[:, h, 0:SPLITS[h], :], wrel_raw[:, 4 * h:4 * h + 4, 0:SPLITS[h]])
            nc.scalar.copy(out=d, in_=s)
            if h == 0:
                nc.scalar.copy(out=bias_sb[:], in_=b_ps[:, 0:16])
            d, s = regroup_views(wrel_grp[:, h, SPLITS[h]:512, :], wrel_raw[:, 4 * h:4 * h + 4, SPLITS[h]:512])
            nc.vector.tensor_copy(out=d, in_=s)
            if h == 0:
                quantise(x_codes[:], x_scales[:], x_grp[:].rearrange("p n t -> p (n t)"))
            quantise(wrel_codes[:, h, :], wrel_scales[:, h, :], wrel_grp[:, h].rearrange("p c t -> p (c t)"))

        wgr_grp = const.tile([P, 3, 128, 4], BF16, align_bytes=64)
        wgr_codes = const.tile([P, 3, 128], I32, align_bytes=64)
        wgr_scales = const.tile([P, 3, 128], U8, align_bytes=64)

        bt_ps = []
        at_sb = const.tile([P, 256, 4], F32)
        bt_sb = const.tile([P, 256, 4], F32)

        head_ps = {}

        def first_relation(a):
            xc, xs = x_codes[:, a * P:(a + 1) * P], x_scales[:, a * P:(a + 1) * P]
            bt_a = atp.tile([P, 4, P], F32, name="bt%d" % a)
            bt_ps.append(bt_a)
            at_tmp = hd.tile([P, 4, P], F32, name="at_tmp", tag="hd")
            bt_tmp = hd.tile([P, 4, P], F32, name="bt_tmp", tag="hd")
            head_ps[a] = (at_tmp, bt_tmp)
            for dst, h in ((at_tmp, 0), (bt_a, 1), (bt_tmp, 1)):
                for t in range(4):
                    mx(dst[:, t, :], wrel_codes[:, h, t * P:(t + 1) * P], wrel_scales[:, h, t * P:(t + 1) * P],
                       xc, xs, True, True)

        def first_relation_out(a):
            at_tmp, bt_tmp = head_ps[a]
            nc.vector.tensor_tensor(
                out=at_sb[:, a * P:(a + 1) * P, :],
                in0=at_tmp[:].rearrange("p t n -> p n t"),
                in1=bias_sb[:, 0:4].unsqueeze(1).to_broadcast([P, P, 4]),
                op=ADD,
            )
            nc.scalar.copy(out=bt_sb[:, a * P:(a + 1) * P, :], in_=bt_tmp[:].rearrange("p t n -> p n t"))

        wgo_grp = const.tile([P, 512, 4], BF16, align_bytes=64)
        for h in range(3):
            d, s = regroup_views(wgr_grp[:, h], wgr_raw[:, 4 * h:4 * h + 4, :])
            nc.scalar.copy(out=d, in_=s)

        first_relation(0)
        first_relation_out(0)
        d, s = regroup_views(wgo_grp[:], wgo_raw[:])
        nc.scalar.copy(out=d, in_=s)

        xj_codes = const.tile([P, 4, 256], I32, align_bytes=64)
        xj_scales = const.tile([P, 4, 256], U8, align_bytes=64)
        nc.vector.tensor_copy(
            out=xj_codes[:].rearrange("p b (i j) -> p b i j", i=4),
            in_=x_codes[:].rearrange("p (b j) -> p b j", b=4).unsqueeze(2).to_broadcast([P, 4, 4, 64]),
        )
        first_relation(1)
        ptb_sb = const.tile([P, 256], F32)

        def second_stage_operands():
            nc.vector.tensor_copy(
                out=xj_scales[:].rearrange("p b c -> p (b c)").bitcast(I32).rearrange(
                    "p (b i j) -> p b i j", b=4, i=4),
                in_=x_scales[:].bitcast(I32).rearrange("p (b j) -> p b j", b=4).unsqueeze(2).to_broadcast(
                    [P, 4, 4, 16]),
            )
            for h in range(3):
                quantise(wgr_codes[:, h, :], wgr_scales[:, h, :], wgr_grp[:, h].rearrange("p c t -> p (c t)"))
            pt_ps = hd.tile([P, 256], F32, tag="hd")
            mx(pt_ps[:], wgr_codes[:, 0, :], wgr_scales[:, 0, :], x_codes[:], x_scales[:], True, True)
            nc.scalar.activation(out=ptb_sb[:], in_=pt_ps[:], func=ACT.Identity, bias=bias_sb[:, 8:9], scale=1.0)

        rel_bf = {}
        rel_codes = {}
        rel_scales = {}
        th_sb = {}

        def build(u, on_gpsimd, slot):
            tok0, n = u
            b = tok0 // 64
            c0 = (b % 2) * 64
            in0 = at_sb[:, tok0:tok0 + n, :].unsqueeze(2).to_broadcast([P, n, 64, 4])
            if on_gpsimd:
                rel_bf[u] = relp.tile([P, n * 256], BF16, name="rel_g", tag=slot, align_bytes=64)
                nc.gpsimd.tensor_tensor(
                    out=rel_bf[u][:].rearrange("p (i j t) -> p i j t", i=n, j=64),
                    in0=in0,
                    in1=bt_sb[:, b * 64:(b + 1) * 64, :].unsqueeze(1).to_broadcast([P, n, 64, 4]),
                    op=ADD,
                )
            else:
                rel_bf[u] = relp.tile([P, n * 256], BF16, name="rel_v", tag=slot, align_bytes=64)
                nc.vector.tensor_tensor(
                    out=rel_bf[u][:].rearrange("p (i j t) -> p i j t", i=n, j=64),
                    in0=in0,
                    in1=bt_ps[b // 2][:, :, c0:c0 + 64].rearrange("p t j -> p j t").unsqueeze(1).to_broadcast(
                        [P, n, 64, 4]),
                    op=ADD,
                )

        planes = {}

        def build_on_scalar(u, i_lo, i_hi):
            tok0, n = u
            b = tok0 // 64
            if i_lo == 0:
                planes[u] = rels.tile([P, 4, n * 64], BF16, name="planes", tag="planes")
                rel_bf[u] = rels.tile([P, n * 256], BF16, name="rel_s", tag="rel_s", align_bytes=64)
            for i in range(i_lo, i_hi):
                for t in range(4):
                    nc.scalar.activation(out=planes[u][:, t, i * 64:(i + 1) * 64],
                                         in_=bt_sb[:, b * 64:(b + 1) * 64, t], func=ACT.Identity,
                                         bias=at_sb[:, tok0 + i, t:t + 1], scale=1.0)
            d, s = regroup_views(
                rel_bf[u][:].rearrange("p (w t) -> p w t", t=4)[:, i_lo * 64:i_hi * 64, :],
                planes[u][:, :, i_lo * 64:i_hi * 64],
            )
            nc.scalar.copy(out=d, in_=s)

        def quant(u):
            n = u[1]
            rel_codes[u] = codp.tile([P, n * 64], I32, name="rel_codes", tag="rel_codes", align_bytes=64)
            rel_scales[u] = codp.tile([P, n * 64], U8, name="rel_scales", tag="rel_scales", align_bytes=64)
            quantise(rel_codes[u][:], rel_scales[u][:], rel_bf[u][:])

        def product(u):
            tok0, n = u
            b = tok0 // 64
            acc = accp.tile([P, n * 64], F32, name="acc", tag="acc")
            for hf in range(n // 4):
                cols = slice(hf * 256, (hf + 1) * 256)
                mx(acc[:, cols], wgr_codes[:, 1, :], wgr_scales[:, 1, :], xj_codes[:, b, :], xj_scales[:, b, :],
                   True, False)
                mx(acc[:, cols], wgr_codes[:, 2, :], wgr_scales[:, 2, :], rel_codes[u][:, cols],
                   rel_scales[u][:, cols], False, True)
            th_sb[u] = thp.tile([P, n * 64], F32, name="th", tag="th")
            for i in range(n):
                tok = tok0 + i
                nc.scalar.activation(out=th_sb[u][:, i * 64:(i + 1) * 64], in_=acc[:, i * 64:(i + 1) * 64],
                                     func=ACT.Tanh, bias=ptb_sb[:, tok:tok + 1], scale=1.0)

        tr_ps = {}

        def turn(u):
            n = u[1]
            tr_ps[u] = trp.tile([P, n * 64], F32, name="tr", tag="tr")
            for k in range(n // 2):
                nc.tensor.transpose(tr_ps[u][:, k * P:(k + 1) * P], th_sb[u][:, k * P:(k + 1) * P], ident_f[:])

        def store(u, on_vector):
            tok0, n = u
            tr = tr_ps[u]
            o_sb = outp.tile([P, n // 2, P], F32, name="o_sb", tag="o_sb")
            if on_vector:
                nc.vector.tensor_copy(out=o_sb[:].rearrange("p k f -> p (k f)"), in_=tr[:])
            else:
                nc.scalar.copy(out=o_sb[:].rearrange("p k f -> p (k f)"), in_=tr[:])
            nc.sync.dma_start(
                out=out1_flat[tok0 * 64:(tok0 + n) * 64, :].rearrange("(k m) f -> m k f", m=P), in_=o_sb[:]
            )

        wgo_codes = const.tile([P, 512], I32, align_bytes=64)
        wgo_scales = const.tile([P, 512], U8, align_bytes=64)
        nxt_sb = const.tile([P, 4, 256], F32)

        def node_update():
            for t in range(4):
                nx_ps = hd.tile([P, 256], F32, name="nx_ps", tag="hd")
                mx(nx_ps[:], wgo_codes[:, t * P:(t + 1) * P], wgo_scales[:, t * P:(t + 1) * P],
                   x_codes[:], x_scales[:], True, True)
                nc.scalar.activation(out=nxt_sb[:, t, :], in_=nx_ps[:], func=ACT.Tanh,
                                     bias=bias_sb[:, 4 + t:5 + t], scale=1.0)
            for a in range(2):
                nxr_ps = hd.tile([P, 512], F32, name="nxr_ps", tag="hd")
                for t in range(4):
                    nc.tensor.transpose(nxr_ps[:, t * P:(t + 1) * P], nxt_sb[:, t, a * P:(a + 1) * P], ident_f[:])
                nx_sb = outp.tile([P, 512], F32, name="nx_sb", tag="nx_sb")
                nc.scalar.copy(out=nx_sb[:], in_=nxr_ps[:])
                nc.sync.dma_start(out=out0_flat[a * P:(a + 1) * P, :], in_=nx_sb[:])

        previous = []
        cycles = schedule()
        last = len(cycles) - 1
        for c, (v_units, g_units, s_units, s_part) in enumerate(cycles):
            units = v_units + s_units + g_units
            slot_g, slot_v2 = ("relZ", "relY") if c % 2 == 0 else ("relY", "relZ")
            for u in g_units:
                build(u, True, slot_g)
            for u, slot in zip(v_units, ("relX", slot_v2)):
                build(u, False, slot)
            if c == 0:
                first_relation_out(1)
                second_stage_operands()
                quantise(wgo_codes[:], wgo_scales[:], wgo_grp[:].rearrange("p c t -> p (c t)"))
            for u in previous:
                turn(u)
                if c < last:
                    store(u, False)
            if s_part is not None:
                build_on_scalar(s_part[0], s_part[1], s_part[2])
            for u in units:
                quant(u)
            for u in units:
                product(u)
            if c == last:
                for u in previous:
                    store(u, True)
                turn(units[0])
                store(units[0], True)
            if c == NODE_AT:
                node_update()
            previous = units
